import numpy as np
import ml_dtypes

BF16 = ml_dtypes.bfloat16


def bf(x):
    return np.asarray(x, np.float32).astype(BF16)


def f32(x):
    return np.asarray(x, np.float32)


def f64(x):
    return np.asarray(x).astype(np.float64)


def striped(idx):
    return np.tile(idx.reshape(-1, 16).T, (8, 1))


C, S, N = 256, 1024, 256


def setup_inputs():
    return {"p_tab": f32(2.0 * np.random.standard_normal((C, S))), "logit": f32(1.5 * np.random.standard_normal((1, N))), "u_emb": f32(0.3 + 0.4 * np.random.standard_normal((C, 1))), "offs": striped(np.random.permutation(S)[:N])}


def reference(p_tab, logit, u_emb, offs):
    idx = offs[:16].T.reshape(-1)
    e = np.exp(f64(logit))
    a = e / e.sum(axis=1, keepdims=True)
    pooled = (f64(p_tab)[:, idx] * a).sum(axis=1, keepdims=True)
    return f64(u_emb) + pooled

@@ -1,0 +1,71 @@
+import concourse.mybir as mybir
+
+F32 = mybir.dt.float32
+U16 = mybir.dt.uint16
+MULT = mybir.AluOpType.mult
+ADD = mybir.AluOpType.add
+EXP = mybir.ActivationFunctionType.Exp
+X = mybir.AxisListType.X
+
+P = 128
+T = 32
+
+
+def tile_acfmodel_kernel(tc, p_tab, logit, u_emb, offs, out):
+    nc = tc.nc
+    C, S = p_tab.shape
+    N = logit.shape[1]
+    B = C // P
+
+    table_blocks = p_tab.rearrange("(b p) s -> b p s", p=P)
+    u_runs = u_emb.rearrange("(b q t) o -> b q (t o)", b=B, t=T)
+    out_runs = out.rearrange("(b q t) o -> b q (t o)", b=B, t=T)
+
+    with tc.tile_pool(name="held", bufs=1) as held:
+        offsets = held.tile([P, N // 16], U16, name="offsets")
+        nc.sync.dma_start(offsets[:], offs)
+
+        scores = held.tile([P, N], F32, name="scores")
+        nc.scalar.dma_start(scores[:], logit.broadcast_to([P, N]))
+
+        tables = [held.tile([P, S], F32, name=f"table{b}") for b in range(B)]
+        nc.sync.dma_start(tables[0][:], table_blocks[0])
+
+        user_runs = held.tile([P, T], F32, name="user_runs", align_bytes=64)
+        nc.gpsimd.memset(user_runs[:], 0.0)
+        for b in range(B):
+            nc.scalar.dma_start(user_runs[b::T, :], u_runs[b])
+        nc.scalar.dma_start(tables[1][:], table_blocks[1])
+        user_cols = held.tile([P, T], F32, name="user_cols", align_bytes=64)
+        nc.vector.transpose(user_cols[:], user_runs[:])
+
+        warm = held.tile([P, 1], F32, name="warm")
+        nc.vector.memset(warm[:], 0.0)
+        nc.scalar.activation(warm[:], warm[:], EXP)
+
+        neg_max = held.tile([P, 1], F32, name="neg_max")
+        nc.vector.reduce_max(neg_max[:], scores[:], X, negate=True)
+        expd = held.tile([P, N], F32, name="expd")
+        exp_sum = held.tile([P, 1], F32, name="exp_sum")
+        nc.scalar.activation(expd[:], scores[:], EXP, bias=neg_max[:], scale=1.0, accum_out=exp_sum[:])
+        inv_sum = held.tile([P, 1], F32, name="inv_sum")
+        nc.vector.reciprocal(inv_sum[:], exp_sum[:])
+
+        store_queues = [nc.scalar, nc.sync]
+        for b in range(B):
+            result_cols = held.tile([P, T], F32, name=f"result_cols{b}", align_bytes=64)
+            nc.vector.memset(result_cols[:], 0.0)
+            weighted = held.tile([P, N], F32, name=f"weighted{b}")
+            nc.vector.tensor_tensor(weighted[:], tables[b][:].indirect(offsets[:]), expd[:], MULT)
+            nc.vector.tensor_scalar(
+                weighted[:],
+                weighted[:],
+                inv_sum[:],
+                user_cols[:, b : b + 1],
+                MULT,
+                ADD,
+                accum_out=result_cols[:, 0:1],
+            )
+            result_runs = held.tile([P, T], F32, name=f"result_runs{b}", align_bytes=64)
+            nc.vector.transpose(result_runs[:], result_cols[:])
+            store_queues[b].dma_start(out_runs[b], result_runs[::T, :])

@@ -17,6 +17,9 @@ def tile_acfmodel_kernel(tc, p_tab, logit, u_emb, offs, out):
     N = logit.shape[1]
     B = C // P
 
+    K = N // T
+    logit_rows = logit.rearrange("o (t k) -> (o t) k", k=K)
+
     table_blocks = p_tab.rearrange("(b p) s -> b p s", p=P)
     u_runs = u_emb.rearrange("(b q t) o -> b q (t o)", b=B, t=T)
     out_runs = out.rearrange("(b q t) o -> b q (t o)", b=B, t=T)
@@ -25,8 +28,9 @@ def tile_acfmodel_kernel(tc, p_tab, logit, u_emb, offs, out):
         offsets = held.tile([P, N // 16], U16, name="offsets")
         nc.sync.dma_start(offsets[:], offs)
 
-        scores = held.tile([P, N], F32, name="scores")
-        nc.scalar.dma_start(scores[:], logit.broadcast_to([P, N]))
+        packed = held.tile([P, K], F32, name="packed")
+        for q in range(P // T):
+            nc.scalar.dma_start(packed[q * T : (q + 1) * T, :], logit_rows)
 
         tables = [held.tile([P, S], F32, name=f"table{b}") for b in range(B)]
         nc.sync.dma_start(tables[0][:], table_blocks[0])
@@ -43,11 +47,25 @@ def tile_acfmodel_kernel(tc, p_tab, logit, u_emb, offs, out):
         nc.vector.memset(warm[:], 0.0)
         nc.scalar.activation(warm[:], warm[:], EXP)
 
+        repeated = held.tile([P, N], F32, name="repeated", align_bytes=64)
+        nc.vector.tensor_copy(
+            repeated[:].rearrange("p (k r) -> p k r", k=K),
+            packed[:].unsqueeze(2).to_broadcast([P, K, T]),
+        )
+        scores = held.tile([P, N], F32, name="scores", align_bytes=64)
+        nc.vector.transpose(scores[:], repeated[:])
         neg_max = held.tile([P, 1], F32, name="neg_max")
         nc.vector.reduce_max(neg_max[:], scores[:], X, negate=True)
         expd = held.tile([P, N], F32, name="expd")
         exp_sum = held.tile([P, 1], F32, name="exp_sum")
-        nc.scalar.activation(expd[:], scores[:], EXP, bias=neg_max[:], scale=1.0, accum_out=exp_sum[:])
+        nc.scalar.activation(
+            expd[:].rearrange("p (t k) -> p t k", k=K),
+            scores[:].rearrange("p (k t) -> p t k", k=K),
+            EXP,
+            bias=neg_max[:],
+            scale=1.0,
+            accum_out=exp_sum[:],
+        )
         inv_sum = held.tile([P, 1], F32, name="inv_sum")
         nc.vector.reciprocal(inv_sum[:], exp_sum[:])
 

@@ -25,12 +25,13 @@ def tile_acfmodel_kernel(tc, p_tab, logit, u_emb, offs, out):
     out_runs = out.rearrange("(b q t) o -> b q (t o)", b=B, t=T)
 
     with tc.tile_pool(name="held", bufs=1) as held:
+        packed = held.tile([P, K], F32, name="packed")
+        load_queues = [nc.sync, nc.scalar]
+        for q in range(P // T):
+            load_queues[q % 2].dma_start(packed[q * T : (q + 1) * T, :], logit_rows)
+
         offsets = held.tile([P, N // 16], U16, name="offsets")
         nc.sync.dma_start(offsets[:], offs)
-
-        packed = held.tile([P, K], F32, name="packed")
-        for q in range(P // T):
-            nc.scalar.dma_start(packed[q * T : (q + 1) * T, :], logit_rows)
 
         tables = [held.tile([P, S], F32, name=f"table{b}") for b in range(B)]
         nc.sync.dma_start(tables[0][:], table_blocks[0])

@@ -5,6 +5,7 @@ U16 = mybir.dt.uint16
 MULT = mybir.AluOpType.mult
 ADD = mybir.AluOpType.add
 EXP = mybir.ActivationFunctionType.Exp
+IDENTITY = mybir.ActivationFunctionType.Identity
 X = mybir.AxisListType.X
 
 P = 128
@@ -76,15 +77,20 @@ def tile_acfmodel_kernel(tc, p_tab, logit, u_emb, offs, out):
             nc.vector.memset(result_cols[:], 0.0)
             weighted = held.tile([P, N], F32, name=f"weighted{b}")
             nc.vector.tensor_tensor(weighted[:], tables[b][:].indirect(offsets[:]), expd[:], MULT)
-            nc.vector.tensor_scalar(
-                weighted[:],
-                weighted[:],
-                inv_sum[:],
-                user_cols[:, b : b + 1],
-                MULT,
-                ADD,
-                accum_out=result_cols[:, 0:1],
-            )
+            if b == 0:
+                pooled = held.tile([P, 1], F32, name="pooled")
+                nc.scalar.activation(weighted[:], weighted[:], IDENTITY, scale=inv_sum[:], accum_out=pooled[:])
+                nc.scalar.activation(result_cols[:, 0:1], pooled[:], IDENTITY, bias=user_cols[:, b : b + 1])
+            else:
+                nc.vector.tensor_scalar(
+                    weighted[:],
+                    weighted[:],
+                    inv_sum[:],
+                    user_cols[:, b : b + 1],
+                    MULT,
+                    ADD,
+                    accum_out=result_cols[:, 0:1],
+                )
             result_runs = held.tile([P, T], F32, name=f"result_runs{b}", align_bytes=64)
             nc.vector.transpose(result_runs[:], result_cols[:])
             store_queues[b].dma_start(out_runs[b], result_runs[::T, :])

@@ -31,11 +31,11 @@ def tile_acfmodel_kernel(tc, p_tab, logit, u_emb, offs, out):
         for q in range(P // T):
             load_queues[q % 2].dma_start(packed[q * T : (q + 1) * T, :], logit_rows)
 
-        offsets = held.tile([P, N // 16], U16, name="offsets")
-        nc.sync.dma_start(offsets[:], offs)
 
         tables = [held.tile([P, S], F32, name=f"table{b}") for b in range(B)]
         nc.sync.dma_start(tables[0][:], table_blocks[0])
+        offsets = held.tile([P, N // 16], U16, name="offsets")
+        nc.sync.dma_start(offsets[:], offs)
 
         user_runs = held.tile([P, T], F32, name="user_runs", align_bytes=64)
         nc.gpsimd.memset(user_runs[:], 0.0)
@@ -44,20 +44,28 @@ def tile_acfmodel_kernel(tc, p_tab, logit, u_emb, offs, out):
         nc.scalar.dma_start(tables[1][:], table_blocks[1])
         user_cols = held.tile([P, T], F32, name="user_cols", align_bytes=64)
         nc.vector.transpose(user_cols[:], user_runs[:])
+        user_share = held.tile([P, 1], F32, name="user_share")
+        nc.gpsimd.tensor_scalar(user_share[:], user_cols[:, 0:1], 1.0 / N, None, MULT)
 
         warm = held.tile([P, 1], F32, name="warm")
         nc.vector.memset(warm[:], 0.0)
         nc.scalar.activation(warm[:], warm[:], EXP)
 
+        own_max = held.tile([P, 1], F32, name="own_max")
+        nc.vector.reduce_max(own_max[:], packed[:], X)
         repeated = held.tile([P, N], F32, name="repeated", align_bytes=64)
         nc.vector.tensor_copy(
             repeated[:].rearrange("p (k r) -> p k r", k=K),
             packed[:].unsqueeze(2).to_broadcast([P, K, T]),
         )
+        own_max_row = held.tile([P, T], F32, name="own_max_row", align_bytes=64)
+        nc.vector.tensor_copy(own_max_row[:], own_max[:].to_broadcast([P, T]))
+        quadrant_max = held.tile([P, T], F32, name="quadrant_max", align_bytes=64)
+        nc.vector.transpose(quadrant_max[:], own_max_row[:])
         scores = held.tile([P, N], F32, name="scores", align_bytes=64)
         nc.vector.transpose(scores[:], repeated[:])
         neg_max = held.tile([P, 1], F32, name="neg_max")
-        nc.vector.reduce_max(neg_max[:], scores[:], X, negate=True)
+        nc.vector.reduce_max(neg_max[:], quadrant_max[:], X, negate=True)
         expd = held.tile([P, N], F32, name="expd")
         exp_sum = held.tile([P, 1], F32, name="exp_sum")
         nc.scalar.activation(
@@ -78,9 +86,14 @@ def tile_acfmodel_kernel(tc, p_tab, logit, u_emb, offs, out):
             weighted = held.tile([P, N], F32, name=f"weighted{b}")
             nc.vector.tensor_tensor(weighted[:], tables[b][:].indirect(offsets[:]), expd[:], MULT)
             if b == 0:
-                pooled = held.tile([P, 1], F32, name="pooled")
-                nc.scalar.activation(weighted[:], weighted[:], IDENTITY, scale=inv_sum[:], accum_out=pooled[:])
-                nc.scalar.activation(result_cols[:, 0:1], pooled[:], IDENTITY, bias=user_cols[:, b : b + 1])
+                nc.scalar.activation(
+                    weighted[:],
+                    weighted[:],
+                    IDENTITY,
+                    bias=user_share[:],
+                    scale=inv_sum[:],
+                    accum_out=result_cols[:, 0:1],
+                )
             else:
                 nc.vector.tensor_scalar(
                     weighted[:],

@@ -22,7 +22,7 @@ def tile_acfmodel_kernel(tc, p_tab, logit, u_emb, offs, out):
     logit_rows = logit.rearrange("o (t k) -> (o t) k", k=K)
 
     table_blocks = p_tab.rearrange("(b p) s -> b p s", p=P)
-    u_runs = u_emb.rearrange("(b q t) o -> b q (t o)", b=B, t=T)
+    u_runs = u_emb.rearrange("(b q t) o -> q b (t o)", b=B, t=T)
     out_runs = out.rearrange("(b q t) o -> b q (t o)", b=B, t=T)
 
     with tc.tile_pool(name="held", bufs=1) as held:
@@ -31,21 +31,21 @@ def tile_acfmodel_kernel(tc, p_tab, logit, u_emb, offs, out):
         for q in range(P // T):
             load_queues[q % 2].dma_start(packed[q * T : (q + 1) * T, :], logit_rows)
 
-
-        tables = [held.tile([P, S], F32, name=f"table{b}") for b in range(B)]
-        nc.sync.dma_start(tables[0][:], table_blocks[0])
         offsets = held.tile([P, N // 16], U16, name="offsets")
         nc.sync.dma_start(offsets[:], offs)
 
-        user_runs = held.tile([P, T], F32, name="user_runs", align_bytes=64)
+        tables = [held.tile([P, S], F32, name=f"table{b}") for b in range(B)]
+        nc.sync.dma_start(tables[0][:], table_blocks[0])
+
+        user_runs = held.tile([P, B * T], F32, name="user_runs", align_bytes=64)
         nc.gpsimd.memset(user_runs[:], 0.0)
-        for b in range(B):
-            nc.scalar.dma_start(user_runs[b::T, :], u_runs[b])
+        nc.scalar.dma_start(user_runs[::T, :].rearrange("q (b t) -> q b t", b=B), u_runs)
         nc.scalar.dma_start(tables[1][:], table_blocks[1])
-        user_cols = held.tile([P, T], F32, name="user_cols", align_bytes=64)
-        nc.vector.transpose(user_cols[:], user_runs[:])
+        user_cols = [held.tile([P, T], F32, name=f"user_cols{b}", align_bytes=64) for b in range(B)]
+        for b in range(B):
+            nc.vector.transpose(user_cols[b][:], user_runs[:, b * T : (b + 1) * T])
         user_share = held.tile([P, 1], F32, name="user_share")
-        nc.gpsimd.tensor_scalar(user_share[:], user_cols[:, 0:1], 1.0 / N, None, MULT)
+        nc.gpsimd.tensor_scalar(user_share[:], user_cols[0][:, 0:1], 1.0 / N, None, MULT)
 
         warm = held.tile([P, 1], F32, name="warm")
         nc.vector.memset(warm[:], 0.0)
@@ -99,7 +99,7 @@ def tile_acfmodel_kernel(tc, p_tab, logit, u_emb, offs, out):
                     weighted[:],
                     weighted[:],
                     inv_sum[:],
-                    user_cols[:, b : b + 1],
+                    user_cols[b][:, 0:1],
                     MULT,
                     ADD,
                     accum_out=result_cols[:, 0:1],

@@ -41,11 +41,6 @@ def tile_acfmodel_kernel(tc, p_tab, logit, u_emb, offs, out):
         nc.gpsimd.memset(user_runs[:], 0.0)
         nc.scalar.dma_start(user_runs[::T, :].rearrange("q (b t) -> q b t", b=B), u_runs)
         nc.scalar.dma_start(tables[1][:], table_blocks[1])
-        user_cols = [held.tile([P, T], F32, name=f"user_cols{b}", align_bytes=64) for b in range(B)]
-        for b in range(B):
-            nc.vector.transpose(user_cols[b][:], user_runs[:, b * T : (b + 1) * T])
-        user_share = held.tile([P, 1], F32, name="user_share")
-        nc.gpsimd.tensor_scalar(user_share[:], user_cols[0][:, 0:1], 1.0 / N, None, MULT)
 
         warm = held.tile([P, 1], F32, name="warm")
         nc.vector.memset(warm[:], 0.0)
@@ -66,6 +61,12 @@ def tile_acfmodel_kernel(tc, p_tab, logit, u_emb, offs, out):
         nc.vector.transpose(scores[:], repeated[:])
         neg_max = held.tile([P, 1], F32, name="neg_max")
         nc.vector.reduce_max(neg_max[:], quadrant_max[:], X, negate=True)
+        user_cols = [held.tile([P, T], F32, name=f"user_cols{b}", align_bytes=64) for b in range(B)]
+        for b in range(B):
+            nc.vector.transpose(user_cols[b][:], user_runs[:, b * T : (b + 1) * T])
+        user_share = held.tile([P, 1], F32, name="user_share")
+        nc.gpsimd.tensor_scalar(user_share[:], user_cols[0][:, 0:1], 1.0 / N, None, MULT)
+
         expd = held.tile([P, N], F32, name="expd")
         exp_sum = held.tile([P, 1], F32, name="exp_sum")
         nc.scalar.activation(

@@ -9,6 +9,7 @@ IDENTITY = mybir.ActivationFunctionType.Identity
 X = mybir.AxisListType.X
 
 P = 128
+H = 2
 T = 32
 
 
@@ -42,6 +43,10 @@ def tile_acfmodel_kernel(tc, p_tab, logit, u_emb, offs, out):
         nc.scalar.dma_start(user_runs[::T, :].rearrange("q (b t) -> q b t", b=B), u_runs)
         nc.scalar.dma_start(tables[1][:], table_blocks[1])
 
+        result_cols = [held.tile([P, T], F32, name=f"result_cols{b}", align_bytes=64) for b in range(B)]
+        for b in range(B):
+            nc.vector.memset(result_cols[b][:], 0.0)
+
         warm = held.tile([P, 1], F32, name="warm")
         nc.vector.memset(warm[:], 0.0)
         nc.scalar.activation(warm[:], warm[:], EXP)
@@ -68,43 +73,55 @@ def tile_acfmodel_kernel(tc, p_tab, logit, u_emb, offs, out):
         nc.gpsimd.tensor_scalar(user_share[:], user_cols[0][:, 0:1], 1.0 / N, None, MULT)
 
         expd = held.tile([P, N], F32, name="expd")
+        exp_sums = held.tile([P, H], F32, name="exp_sums")
+        scores_in_order = scores[:].rearrange("p (k t) -> p t k", k=K)
+        expd_in_order = expd[:].rearrange("p (t k) -> p t k", k=K)
+        for h in range(H):
+            half = slice(h * T // H, (h + 1) * T // H)
+            nc.scalar.activation(
+                expd_in_order[:, half, :],
+                scores_in_order[:, half, :],
+                EXP,
+                bias=neg_max[:],
+                scale=1.0,
+                accum_out=exp_sums[:, h : h + 1],
+            )
         exp_sum = held.tile([P, 1], F32, name="exp_sum")
-        nc.scalar.activation(
-            expd[:].rearrange("p (t k) -> p t k", k=K),
-            scores[:].rearrange("p (k t) -> p t k", k=K),
-            EXP,
-            bias=neg_max[:],
-            scale=1.0,
-            accum_out=exp_sum[:],
-        )
+        nc.gpsimd.tensor_tensor(exp_sum[:], exp_sums[:, 0:1], exp_sums[:, 1:2], ADD)
+
+        weighted = [held.tile([P, N], F32, name=f"weighted{b}") for b in range(B)]
+        for h in range(H):
+            half = slice(h * N // H, (h + 1) * N // H)
+            nc.vector.tensor_tensor(
+                weighted[0][:, half],
+                tables[0][:].indirect(offsets[:, h * N // H // 16 : (h + 1) * N // H // 16]),
+                expd[:, half],
+                MULT,
+            )
         inv_sum = held.tile([P, 1], F32, name="inv_sum")
         nc.vector.reciprocal(inv_sum[:], exp_sum[:])
+        nc.vector.tensor_tensor(weighted[1][:], tables[1][:].indirect(offsets[:]), expd[:], MULT)
+
+        nc.scalar.activation(
+            weighted[0][:],
+            weighted[0][:],
+            IDENTITY,
+            bias=user_share[:],
+            scale=inv_sum[:],
+            accum_out=result_cols[0][:, 0:1],
+        )
+        nc.vector.tensor_scalar(
+            weighted[1][:],
+            weighted[1][:],
+            inv_sum[:],
+            user_cols[1][:, 0:1],
+            MULT,
+            ADD,
+            accum_out=result_cols[1][:, 0:1],
+        )
 
         store_queues = [nc.scalar, nc.sync]
         for b in range(B):
-            result_cols = held.tile([P, T], F32, name=f"result_cols{b}", align_bytes=64)
-            nc.vector.memset(result_cols[:], 0.0)
-            weighted = held.tile([P, N], F32, name=f"weighted{b}")
-            nc.vector.tensor_tensor(weighted[:], tables[b][:].indirect(offsets[:]), expd[:], MULT)
-            if b == 0:
-                nc.scalar.activation(
-                    weighted[:],
-                    weighted[:],
-                    IDENTITY,
-                    bias=user_share[:],
-                    scale=inv_sum[:],
-                    accum_out=result_cols[:, 0:1],
-                )
-            else:
-                nc.vector.tensor_scalar(
-                    weighted[:],
-                    weighted[:],
-                    inv_sum[:],
-                    user_cols[b][:, 0:1],
-                    MULT,
-                    ADD,
-                    accum_out=result_cols[:, 0:1],
-                )
             result_runs = held.tile([P, T], F32, name=f"result_runs{b}", align_bytes=64)
-            nc.vector.transpose(result_runs[:], result_cols[:])
+            nc.vector.transpose(result_runs[:], result_cols[b][:])
             store_queues[b].dma_start(out_runs[b], result_runs[::T, :])

@@ -70,7 +70,7 @@ def tile_acfmodel_kernel(tc, p_tab, logit, u_emb, offs, out):
         for b in range(B):
             nc.vector.transpose(user_cols[b][:], user_runs[:, b * T : (b + 1) * T])
         user_share = held.tile([P, 1], F32, name="user_share")
-        nc.gpsimd.tensor_scalar(user_share[:], user_cols[0][:, 0:1], 1.0 / N, None, MULT)
+        nc.vector.tensor_scalar(user_share[:], user_cols[0][:, 0:1], 1.0 / N, None, MULT)
 
         expd = held.tile([P, N], F32, name="expd")
         exp_sums = held.tile([P, H], F32, name="exp_sums")
@@ -87,7 +87,7 @@ def tile_acfmodel_kernel(tc, p_tab, logit, u_emb, offs, out):
                 accum_out=exp_sums[:, h : h + 1],
             )
         exp_sum = held.tile([P, 1], F32, name="exp_sum")
-        nc.gpsimd.tensor_tensor(exp_sum[:], exp_sums[:, 0:1], exp_sums[:, 1:2], ADD)
+        nc.scalar.activation(exp_sum[:], exp_sums[:, 0:1], IDENTITY, bias=exp_sums[:, 1:2])
 
         weighted = [held.tile([P, N], F32, name=f"weighted{b}") for b in range(B)]
         for h in range(H):

import concourse.mybir as mybir

F32 = mybir.dt.float32
U16 = mybir.dt.uint16
MULT = mybir.AluOpType.mult
ADD = mybir.AluOpType.add
EXP = mybir.ActivationFunctionType.Exp
IDENTITY = mybir.ActivationFunctionType.Identity
X = mybir.AxisListType.X

P = 128
H = 2
T = 32


def tile_acfmodel_kernel(tc, p_tab, logit, u_emb, offs, out):
    nc = tc.nc
    C, S = p_tab.shape
    N = logit.shape[1]
    B = C // P

    K = N // T
    logit_rows = logit.rearrange("o (t k) -> (o t) k", k=K)

    table_blocks = p_tab.rearrange("(b p) s -> b p s", p=P)
    u_runs = u_emb.rearrange("(b q t) o -> q b (t o)", b=B, t=T)
    out_runs = out.rearrange("(b q t) o -> b q (t o)", b=B, t=T)

    with tc.tile_pool(name="held", bufs=1) as held:
        packed = held.tile([P, K], F32, name="packed")
        load_queues = [nc.sync, nc.scalar]
        for q in range(P // T):
            load_queues[q % 2].dma_start(packed[q * T : (q + 1) * T, :], logit_rows)

        offsets = held.tile([P, N // 16], U16, name="offsets")
        nc.sync.dma_start(offsets[:], offs)

        tables = [held.tile([P, S], F32, name=f"table{b}") for b in range(B)]
        nc.sync.dma_start(tables[0][:], table_blocks[0])

        user_runs = held.tile([P, B * T], F32, name="user_runs", align_bytes=64)
        nc.gpsimd.memset(user_runs[:], 0.0)
        nc.scalar.dma_start(user_runs[::T, :].rearrange("q (b t) -> q b t", b=B), u_runs)
        nc.scalar.dma_start(tables[1][:], table_blocks[1])

        result_cols = [held.tile([P, T], F32, name=f"result_cols{b}", align_bytes=64) for b in range(B)]
        for b in range(B):
            nc.vector.memset(result_cols[b][:], 0.0)

        warm = held.tile([P, 1], F32, name="warm")
        nc.vector.memset(warm[:], 0.0)
        nc.scalar.activation(warm[:], warm[:], EXP)

        own_max = held.tile([P, 1], F32, name="own_max")
        nc.vector.reduce_max(own_max[:], packed[:], X)
        repeated = held.tile([P, N], F32, name="repeated", align_bytes=64)
        nc.vector.tensor_copy(
            repeated[:].rearrange("p (k r) -> p k r", k=K),
            packed[:].unsqueeze(2).to_broadcast([P, K, T]),
        )
        own_max_row = held.tile([P, T], F32, name="own_max_row", align_bytes=64)
        nc.vector.tensor_copy(own_max_row[:], own_max[:].to_broadcast([P, T]))
        quadrant_max = held.tile([P, T], F32, name="quadrant_max", align_bytes=64)
        nc.vector.transpose(quadrant_max[:], own_max_row[:])
        scores = held.tile([P, N], F32, name="scores", align_bytes=64)
        nc.vector.transpose(scores[:], repeated[:])
        neg_max = held.tile([P, 1], F32, name="neg_max")
        nc.vector.reduce_max(neg_max[:], quadrant_max[:], X, negate=True)
        user_cols = [held.tile([P, T], F32, name=f"user_cols{b}", align_bytes=64) for b in range(B)]
        for b in range(B):
            nc.vector.transpose(user_cols[b][:], user_runs[:, b * T : (b + 1) * T])
        user_share = held.tile([P, 1], F32, name="user_share")
        nc.vector.tensor_scalar(user_share[:], user_cols[0][:, 0:1], 1.0 / N, None, MULT)

        expd = held.tile([P, N], F32, name="expd")
        exp_sums = held.tile([P, H], F32, name="exp_sums")
        scores_in_order = scores[:].rearrange("p (k t) -> p t k", k=K)
        expd_in_order = expd[:].rearrange("p (t k) -> p t k", k=K)
        for h in range(H):
            half = slice(h * T // H, (h + 1) * T // H)
            nc.scalar.activation(
                expd_in_order[:, half, :],
                scores_in_order[:, half, :],
                EXP,
                bias=neg_max[:],
                scale=1.0,
                accum_out=exp_sums[:, h : h + 1],
            )
        exp_sum = held.tile([P, 1], F32, name="exp_sum")
        nc.scalar.activation(exp_sum[:], exp_sums[:, 0:1], IDENTITY, bias=exp_sums[:, 1:2])

        weighted = [held.tile([P, N], F32, name=f"weighted{b}") for b in range(B)]
        for h in range(H):
            half = slice(h * N // H, (h + 1) * N // H)
            nc.vector.tensor_tensor(
                weighted[0][:, half],
                tables[0][:].indirect(offsets[:, h * N // H // 16 : (h + 1) * N // H // 16]),
                expd[:, half],
                MULT,
            )
        inv_sum = held.tile([P, 1], F32, name="inv_sum")
        nc.vector.reciprocal(inv_sum[:], exp_sum[:])
        nc.vector.tensor_tensor(weighted[1][:], tables[1][:].indirect(offsets[:]), expd[:], MULT)

        nc.scalar.activation(
            weighted[0][:],
            weighted[0][:],
            IDENTITY,
            bias=user_share[:],
            scale=inv_sum[:],
            accum_out=result_cols[0][:, 0:1],
        )
        nc.vector.tensor_scalar(
            weighted[1][:],
            weighted[1][:],
            inv_sum[:],
            user_cols[1][:, 0:1],
            MULT,
            ADD,
            accum_out=result_cols[1][:, 0:1],
        )

        store_queues = [nc.scalar, nc.sync]
        for b in range(B):
            result_runs = held.tile([P, T], F32, name=f"result_runs{b}", align_bytes=64)
            nc.vector.transpose(result_runs[:], result_cols[b][:])
            store_queues[b].dma_start(out_runs[b], result_runs[::T, :])
